import numpy as np
import ml_dtypes


def mxq(x, axis, fmt="e4m3"):
    dtype, down = {"e4m3": (ml_dtypes.float8_e4m3fn, 7), "e5m2": (ml_dtypes.float8_e5m2, 14)}[fmt]
    v = np.moveaxis(np.asarray(x, np.float32).astype(ml_dtypes.bfloat16).astype(np.float64), axis, -1)
    blocks = v.reshape(v.shape[:-1] + (-1, 32))
    amax = np.abs(blocks).max(-1, keepdims=True)
    byte = np.maximum(np.where(amax > 0, np.frexp(amax)[1] - 1 + 127, 0) - down, 1)
    scale = np.exp2(byte - 127.0)
    codes = (blocks / scale).astype(np.float32).astype(dtype).astype(np.float64)
    return np.moveaxis((codes * scale).reshape(v.shape), -1, axis)


WIDE = False


def mx_kscale(k):
    if not WIDE:
        return np.ones(k)
    levels = np.array([30, -30])
    if k % 512:
        return np.exp2(np.random.permutation(np.resize(levels, k // 32))).repeat(32)
    a = np.empty((k // 512, 16))
    for p in range(k // 512):
        a[p, :8] = np.random.permutation(np.resize(levels, 8))
        for g in range(8):
            far = levels[np.abs(levels - a[p, g]) >= 10]
            a[p, g + 8] = far[np.random.randint(len(far))]
    return np.exp2(a.ravel()).repeat(32)


BF16 = ml_dtypes.bfloat16


def bf(x):
    return np.asarray(x, np.float32).astype(BF16)


def f64(x):
    return np.asarray(x).astype(np.float64)


B, T, C, H, G, D = 2, 512, 1024, 8, 2, 128
EPS = 1e-6


def rmsnorm(v, w):
    return v / np.sqrt(np.mean(v * v, axis=-1, keepdims=True) + EPS) * w


def apply_rotary(v, cos, sin):
    v1, v2 = np.split(v, 2, axis=-1)
    return np.concatenate([v1 * cos - v2 * sin, v1 * sin + v2 * cos], axis=-1)


def setup_inputs():
    s = mx_kscale(C)
    ang = np.arange(T)[:, None] / 10000.0 ** (np.arange(0, D, 2) / D)[None, :]
    a = 4.0 * np.sqrt(EPS / C)
    return {"x": bf(np.random.standard_normal((B, T, C)) * s),
            "cos": bf(np.cos(ang)[None, None, :, :]),
            "sin": bf(np.sin(ang)[None, None, :, :]),
            "wq": bf(np.random.standard_normal((G * H * D, C)) * a / s[None, :]),
            "wk": bf(np.random.standard_normal((H * D, C)) * a / s[None, :]),
            "wv": bf(np.random.standard_normal((H * D, C)) / np.sqrt(C) / s[None, :]),
            "q_norm_w": bf(1.0 + 0.1 * np.random.standard_normal(D)),
            "k_norm_w": bf(1.0 + 0.1 * np.random.standard_normal(D))}


def reference(x, cos, sin, wq, wk, wv, q_norm_w, k_norm_w):
    xq = mxq(f64(x), 2, "e5m2")
    q = (xq @ mxq(f64(wq), 1, "e5m2").T).reshape(B, T, G * H, D).transpose(0, 2, 1, 3)
    k = (xq @ mxq(f64(wk), 1, "e5m2").T).reshape(B, T, H, D).transpose(0, 2, 1, 3)
    v = (xq @ mxq(f64(wv), 1, "e5m2").T).reshape(B, T, H, D).transpose(0, 2, 1, 3)
    q = rmsnorm(q, f64(q_norm_w))
    k = rmsnorm(k, f64(k_norm_w))
    c, sn = f64(cos)[:, :, :T, :], f64(sin)[:, :, :T, :]
    q = apply_rotary(q, c, sn)
    k = apply_rotary(k, c, sn)
    return q, k, v

@@ -1,0 +1,308 @@
+from contextlib import ExitStack
+
+import concourse.mybir as mybir
+from concourse.masks import make_identity
+
+B, T, C, D = 2, 512, 1024, 128
+EPS = 1e-6
+FLOPS = 2 * B * T * C * 4096
+
+F32 = mybir.dt.float32
+BF16 = mybir.dt.bfloat16
+U32 = mybir.dt.uint32
+U8 = mybir.dt.uint8
+E5M2X4 = mybir.dt.float8_e5m2_x4
+ACT = mybir.ActivationFunctionType
+ALU = mybir.AluOpType
+
+P = 128
+J = T // P
+HEADS = 4
+N = HEADS * D
+PASSES = C // 512
+HALF = D // 2
+QK_CHUNKS = 6
+STEPS = QK_CHUNKS * B * J
+ROW_BUFS = 20
+
+
+def tile_qwen3attention_pa_kernel(tc, x, cos, sin, wq, wk, wv, q_norm_w, k_norm_w, out_0, out_1, out_2):
+    nc = tc.nc
+    with ExitStack() as ctx:
+        const = ctx.enter_context(tc.tile_pool(name="const", bufs=1))
+        work = ctx.enter_context(tc.tile_pool(name="work", bufs=2))
+        psum = ctx.enter_context(tc.psum_pool(name="psum", bufs=4))
+        ctx.enter_context(tc.manual_schedule())
+
+        def weight_rows(name):
+            kind, c = name
+            if kind == "v":
+                return wv[c * N : (c + 1) * N, :]
+            if c < 4:
+                return wq[c * N : (c + 1) * N, :]
+            return wk[(c - 4) * N : (c - 3) * N, :]
+
+        def hbm_rows(item):
+            name, r = item
+            if name[0] == "x":
+                return x[name[1]].rearrange("(p j) k -> p j k", j=J)[:, r, :]
+            return weight_rows(name)[r * P : (r + 1) * P, :]
+
+        def group(name):
+            return [(name, r) for r in range(4)]
+
+        later = [("qk", 1), ("v", 0), ("qk", 2), ("qk", 3), ("qk", 4), ("v", 1), ("qk", 5)]
+        load_order = group(("x", 0))[:1] + group(("qk", 0)) + group(("x", 0))[1:] + group(("x", 1))
+        for name in later:
+            load_order = load_order + group(name)
+        rows = {}
+        banks = {}
+        grouped = {}
+        codes = {}
+        scales = {}
+
+        def load_next():
+            if len(rows) < len(load_order):
+                item = load_order[len(rows)]
+                raw = work.tile([P, C], BF16, tag="rows", bufs=ROW_BUFS, name="raw")
+                nc.sync.dma_start(out=raw[:], in_=hbm_rows(item))
+                rows[item] = raw
+
+        def transpose_rows(item):
+            words = rows[item][:].bitcast(F32)
+            bank = psum.tile([P, PASSES, 2, P], F32, tag="side", name="turned")
+            for g in range(PASSES):
+                for u in range(2):
+                    nc.tensor.transpose(bank[:, g, u, :], words[:, 256 * g + u : 256 * (g + 1) : 2], ident[:])
+            banks[item] = bank
+            load_next()
+
+        def interleave(item, on_vector=False):
+            name, r = item
+            if name not in grouped:
+                staged = work.tile([P, 4 * C], BF16, tag="grouped", bufs=3, align_bytes=64, name="staged")
+                grouped[name] = staged
+            words = grouped[name][:].bitcast(F32)
+            if name[0] == "x":
+                dst = words.rearrange("p (r g n u) -> p r g n u", r=4, g=PASSES, u=2)[:, r]
+            else:
+                dst = words.rearrange("p (g r n u) -> p g r n u", r=4, g=PASSES, u=2)[:, :, r]
+            src = banks[item][:].rearrange("p g u n -> p g n u")
+            if on_vector:
+                nc.vector.tensor_copy(out=dst, in_=src)
+            else:
+                nc.scalar.copy(out=dst, in_=src)
+
+        def quantize(name, first, last):
+            if name not in codes:
+                code_tile = work.tile([P, C], U32, tag="codes_" + name[0], align_bytes=64, name="code_tile")
+                scale_tile = work.tile([P, C], U8, tag="scales_" + name[0], align_bytes=64, name="scale_tile")
+                codes[name] = code_tile
+                scales[name] = scale_tile
+            cols = slice(256 * first, 256 * last)
+            nc.vector.quantize_mx(
+                out=codes[name][:, cols].bitcast(E5M2X4),
+                scales=scales[name][:, cols],
+                in_=grouped[name][:, C * first : C * last],
+            )
+
+        def project(name, b, j, tag):
+            bank = psum.tile([P, N], F32, tag=tag, name="sums")
+            for g in range(PASSES):
+                tok = slice((j * PASSES + g) * P, (j * PASSES + g + 1) * P)
+                ch = slice(g * N, (g + 1) * N)
+                nc.tensor.matmul_mx(
+                    out=bank[:],
+                    lhsT=codes[("x", b)][:, tok].bitcast(E5M2X4),
+                    lhsT_scale=scales[("x", b)][:, tok],
+                    rhs=codes[name][:, ch].bitcast(E5M2X4),
+                    rhs_scale=scales[name][:, ch],
+                    start=(g == 0),
+                    stop=(g == PASSES - 1),
+                )
+            return bank
+
+        def place(s):
+            return s // (B * J), (s // J) % B, s % J
+
+        sums = {}
+        square_sums = {}
+        rstd = {}
+        products = {}
+        v_staged = {}
+
+        def project_qk(s):
+            c, b, j = place(s)
+            sums[s] = project(("qk", c), b, j, "main")
+
+        def squares(s):
+            ss = work.tile([P, HEADS], F32, tag="ss", bufs=4, name="ss")
+            squared = work.tile([P, N], BF16, tag="squared", name="squared")
+            for h in range(HEADS):
+                nc.scalar.activation(
+                    out=squared[:, h * D : (h + 1) * D],
+                    in_=sums[s][:, h * D : (h + 1) * D],
+                    func=ACT.Square,
+                    accum_out=ss[:, h : h + 1],
+                )
+            square_sums[s] = ss
+
+        def inverse_rms(s):
+            inv = work.tile([P, HEADS], F32, tag="rstd", bufs=4, name="inv")
+            nc.scalar.activation(
+                out=inv[:], in_=square_sums[s][:], func=ACT.Abs_reciprocal_sqrt, scale=1.0 / (D * EPS), bias=1.0
+            )
+            rstd[s] = inv
+
+        def multiply(s):
+            c, b, j = place(s)
+            if j == 0:
+                prod = work.tile([P, HEADS, J, 2, D], F32, tag="products", bufs=3, name="prod")
+                products[(c, b)] = prod
+            table = tables[0 if c < 4 else 1]
+            by_head = sums[s][:].rearrange("p (h d) -> p h d", h=HEADS)
+            for h in range(HEADS):
+                nc.vector.scalar_tensor_tensor(
+                    out=products[(c, b)][:, h, j],
+                    in0=by_head[:, h : h + 1, :].to_broadcast([P, 2, D]),
+                    scalar=rstd[s][:, h : h + 1],
+                    in1=table[:, j],
+                    op0=ALU.mult,
+                    op1=ALU.mult,
+                )
+
+        def hbm_heads(out, first_head, b):
+            return out[b, first_head : first_head + HEADS].rearrange("h (p j) d -> p h (j d)", j=J)
+
+        def add_and_store(c, b):
+            done = work.tile([P, HEADS, J * D], F32, tag="done", bufs=3, name="done")
+            terms = products[(c, b)][:].rearrange("p h j a (e i) -> p h (j a) e i", e=2)
+            total = done[:].rearrange("p h (m i) -> p h m i", i=HALF)
+            dst = hbm_heads(out_0, HEADS * c, b) if c < 4 else hbm_heads(out_1, HEADS * (c - 4), b)
+            if (c, b) == (QK_CHUNKS - 1, B - 1):
+                for h in range(HEADS):
+                    nc.vector.tensor_tensor(out=total[:, h], in0=terms[:, h, :, 0, :], in1=terms[:, h, :, 1, :], op=ALU.add)
+                    nc.sync.dma_start(out=dst[:, h, :], in_=done[:, h, :])
+            else:
+                nc.gpsimd.tensor_tensor(out=total, in0=terms[:, :, :, 0, :], in1=terms[:, :, :, 1, :], op=ALU.add)
+                nc.sync.dma_start(out=dst, in_=done[:])
+
+        def produce(job):
+            if job[0] == "rows":
+                transpose_rows(job[1])
+            else:
+                c, b, j = job[1]
+                banks[job] = project(("v", c), b, j, "side")
+
+        def consume(job):
+            if job[0] == "rows":
+                interleave(job[1])
+                return
+            c, b, j = job[1]
+            if j == 0:
+                values = work.tile([P, HEADS, J, D], F32, tag="values", name="values")
+                v_staged[(c, b)] = values
+            nc.scalar.copy(out=v_staged[(c, b)][:, :, j, :], in_=banks[job][:].rearrange("p (h d) -> p h d", h=HEADS))
+            if j == J - 1:
+                nc.sync.dma_start(
+                    out=hbm_heads(out_2, HEADS * c, b), in_=v_staged[(c, b)][:].rearrange("p h j d -> p h (j d)")
+                )
+
+        ident = const.tile([P, P], F32)
+        make_identity(nc, ident[:])
+        gain_row = const.tile([P, 2 * D], BF16)
+        ones = const.tile([P, P], BF16)
+        nc.vector.memset(gain_row[:], 0.0)
+        nc.vector.memset(ones[:], 1.0)
+        cos_sb = const.tile([P, J, HALF], BF16)
+        sin_sb = const.tile([P, J, HALF], BF16)
+        nc.scalar.dma_start(out=gain_row[0:1, 0:D], in_=q_norm_w.rearrange("(o d) -> o d", o=1))
+        nc.scalar.dma_start(out=gain_row[0:1, D : 2 * D], in_=k_norm_w.rearrange("(o d) -> o d", o=1))
+        nc.scalar.dma_start(out=cos_sb[:], in_=cos[0, 0].rearrange("(p j) f -> p j f", j=J))
+        nc.scalar.dma_start(out=sin_sb[:], in_=sin[0, 0].rearrange("(p j) f -> p j f", j=J))
+        for item in load_order[:ROW_BUFS]:
+            load_next()
+
+        gains = psum.tile([P, 4, HALF], F32, tag="main", name="gains")
+        nc.tensor.matmul(gains[:].rearrange("p e i -> p (e i)"), lhsT=ones[:], rhs=gain_row[:], start=True, stop=True)
+        tables = []
+        for which in range(2):
+            table = const.tile([P, J, 2, D], F32, name="table%d" % which)
+            tables.append(table)
+            for a in range(2):
+                for e in range(2):
+                    nc.vector.scalar_tensor_tensor(
+                        out=table[:, :, a, e * HALF : (e + 1) * HALF],
+                        in0=gains[:, 2 * which + e : 2 * which + e + 1, :].to_broadcast([P, J, HALF]),
+                        scalar=(-1.0 if (a, e) == (0, 1) else 1.0) * EPS**-0.5,
+                        in1=(cos_sb if a == e else sin_sb)[:],
+                        op0=ALU.mult,
+                        op1=ALU.mult,
+                    )
+
+        x0, x1, w0 = ("x", 0), ("x", 1), ("qk", 0)
+        transpose_rows((x0, 0))
+        interleave((x0, 0))
+        quantize(x0, 0, 1)
+        for r in range(HEADS):
+            transpose_rows((w0, r))
+            interleave((w0, r), on_vector=(r % 2 == 1))
+        transpose_rows((x0, 1))
+        interleave((x0, 1))
+        quantize(w0, 0, 2)
+        quantize(w0, 2, 4)
+        quantize(x0, 1, 2)
+        project_qk(0)
+        project_qk(1)
+        for r in (2, 3):
+            transpose_rows((x0, r))
+            interleave((x0, r), on_vector=True)
+        quantize(x0, 2, 4)
+
+        jobs = {s: [] for s in range(-1, STEPS + 1)}
+        quantize_after = {0: (x1, 0, 2), 1: (x1, 2, 4)}
+        first = group(x1) + group(later[0])
+        for i, item in enumerate(first):
+            jobs[i // 2 - 1].append(("rows", item))
+        quantize_after[J - 1] = (later[0], 0, 4)
+        quads = [later[1], later[2], (0, 0), later[3], (0, 1), later[4], later[5], later[6], (1, 0), (1, 1)]
+        for q, what in enumerate(quads):
+            for i in range(J):
+                s = J * (q + 1) - 1 + i
+                if isinstance(what[0], str):
+                    jobs[s].append(("rows", (what, i)))
+                    quantize_after[J * (q + 2) - 1] = (what, 0, 4)
+                else:
+                    jobs[s].append(("v", (what[0], what[1], i)))
+
+        made = set()
+
+        def produce_for(s):
+            for job in jobs[s]:
+                if job not in made:
+                    produce(job)
+                    made.add(job)
+                    if job[0] == "rows" and len(jobs[s]) == 1 and job[1][1] % 2 == 0:
+                        produce(jobs[s + 1][0])
+                        made.add(jobs[s + 1][0])
+
+        produce_for(-1)
+        for s in range(-1, STEPS):
+            if 2 <= s + 2 < STEPS:
+                project_qk(s + 2)
+            produce_for(s + 1)
+            if s + 1 < STEPS:
+                squares(s + 1)
+            for job in jobs[s][:1]:
+                consume(job)
+            if s + 1 < STEPS:
+                inverse_rms(s + 1)
+            for job in jobs[s][1:]:
+                consume(job)
+            if s >= 0:
+                multiply(s)
+                if s in quantize_after:
+                    quantize(*quantize_after[s])
+                if s % J == J - 1:
+                    c, b, j = place(s)
+                    add_and_store(c, b)

@@ -5,7 +5,7 @@ from concourse.masks import make_identity
 
 B, T, C, D = 2, 512, 1024, 128
 EPS = 1e-6
-FLOPS = 2 * B * T * C * 4096
+FLOPS = 2 * B * T * C * (16 + 8 + 8) * D
 
 F32 = mybir.dt.float32
 BF16 = mybir.dt.bfloat16
@@ -20,9 +20,10 @@ J = T // P
 HEADS = 4
 N = HEADS * D
 PASSES = C // 512
+PASS_WORDS = 256
 HALF = D // 2
-QK_CHUNKS = 6
-STEPS = QK_CHUNKS * B * J
+Q_CHUNKS, K_CHUNKS, V_CHUNKS = 4, 2, 2
+STEPS = (Q_CHUNKS + K_CHUNKS) * B * J
 ROW_BUFS = 20
 
 
@@ -34,89 +35,89 @@ def tile_qwen3attention_pa_kernel(tc, x, cos, sin, wq, wk, wv, q_norm_w, k_norm_
         psum = ctx.enter_context(tc.psum_pool(name="psum", bufs=4))
         ctx.enter_context(tc.manual_schedule())
 
-        def weight_rows(name):
-            kind, c = name
+        def row_tiles(operand):
+            return [(operand, r) for r in range(4)]
+
+        def hbm_rows(row_tile):
+            (kind, i), r = row_tile
+            if kind == "x":
+                return x[i].rearrange("(p j) k -> p j k", j=J)[:, r, :]
             if kind == "v":
-                return wv[c * N : (c + 1) * N, :]
-            if c < 4:
-                return wq[c * N : (c + 1) * N, :]
-            return wk[(c - 4) * N : (c - 3) * N, :]
+                return wv[i * N + r * D : i * N + (r + 1) * D, :]
+            if i < Q_CHUNKS:
+                return wq[i * N + r * D : i * N + (r + 1) * D, :]
+            return wk[(i - Q_CHUNKS) * N + r * D : (i - Q_CHUNKS) * N + (r + 1) * D, :]
 
-        def hbm_rows(item):
-            name, r = item
-            if name[0] == "x":
-                return x[name[1]].rearrange("(p j) k -> p j k", j=J)[:, r, :]
-            return weight_rows(name)[r * P : (r + 1) * P, :]
+        def hbm_heads(out, chunk, b):
+            return out[b, HEADS * chunk : HEADS * (chunk + 1)].rearrange("h (p j) d -> p h (j d)", j=J)
 
-        def group(name):
-            return [(name, r) for r in range(4)]
+        x0, x1, w0, w1 = ("x", 0), ("x", 1), ("qk", 0), ("qk", 1)
+        side_work = [("v", 0), ("qk", 2), (0, 0), ("qk", 3), ("v", 1), ("qk", 4), (0, 1), ("qk", 5), (1, 0), (1, 1)]
+        load_order = row_tiles(x0)[:1] + row_tiles(w0) + row_tiles(x0)[1:] + row_tiles(x1) + row_tiles(w1)
+        for what in side_work:
+            if isinstance(what[0], str):
+                load_order = load_order + row_tiles(what)
 
-        later = [("qk", 1), ("v", 0), ("qk", 2), ("qk", 3), ("qk", 4), ("v", 1), ("qk", 5)]
-        load_order = group(("x", 0))[:1] + group(("qk", 0)) + group(("x", 0))[1:] + group(("x", 1))
-        for name in later:
-            load_order = load_order + group(name)
-        rows = {}
-        banks = {}
-        grouped = {}
+        loaded = {}
+        side_banks = {}
+        interleaved = {}
         codes = {}
         scales = {}
 
         def load_next():
-            if len(rows) < len(load_order):
-                item = load_order[len(rows)]
+            if len(loaded) < len(load_order):
+                row_tile = load_order[len(loaded)]
                 raw = work.tile([P, C], BF16, tag="rows", bufs=ROW_BUFS, name="raw")
-                nc.sync.dma_start(out=raw[:], in_=hbm_rows(item))
-                rows[item] = raw
+                nc.sync.dma_start(out=raw[:], in_=hbm_rows(row_tile))
+                loaded[row_tile] = raw
 
-        def transpose_rows(item):
-            words = rows[item][:].bitcast(F32)
+        def transpose_rows(row_tile):
+            words = loaded[row_tile][:].bitcast(F32)
             bank = psum.tile([P, PASSES, 2, P], F32, tag="side", name="turned")
             for g in range(PASSES):
                 for u in range(2):
-                    nc.tensor.transpose(bank[:, g, u, :], words[:, 256 * g + u : 256 * (g + 1) : 2], ident[:])
-            banks[item] = bank
+                    nc.tensor.transpose(
+                        bank[:, g, u, :], words[:, PASS_WORDS * g + u : PASS_WORDS * (g + 1) : 2], ident[:]
+                    )
+            side_banks[row_tile] = bank
             load_next()
 
-        def interleave(item, on_vector=False):
-            name, r = item
-            if name not in grouped:
-                staged = work.tile([P, 4 * C], BF16, tag="grouped", bufs=3, align_bytes=64, name="staged")
-                grouped[name] = staged
-            words = grouped[name][:].bitcast(F32)
-            if name[0] == "x":
+        def interleave(row_tile, copy):
+            operand, r = row_tile
+            if operand not in interleaved:
+                staged = work.tile([P, 4 * C], BF16, tag="interleaved", bufs=3, align_bytes=64, name="staged")
+                interleaved[operand] = staged
+            words = interleaved[operand][:].bitcast(F32)
+            if operand[0] == "x":
                 dst = words.rearrange("p (r g n u) -> p r g n u", r=4, g=PASSES, u=2)[:, r]
             else:
                 dst = words.rearrange("p (g r n u) -> p g r n u", r=4, g=PASSES, u=2)[:, :, r]
-            src = banks[item][:].rearrange("p g u n -> p g n u")
-            if on_vector:
-                nc.vector.tensor_copy(out=dst, in_=src)
-            else:
-                nc.scalar.copy(out=dst, in_=src)
+            copy(out=dst, in_=side_banks[row_tile][:].rearrange("p g u n -> p g n u"))
 
-        def quantize(name, first, last):
-            if name not in codes:
-                code_tile = work.tile([P, C], U32, tag="codes_" + name[0], align_bytes=64, name="code_tile")
-                scale_tile = work.tile([P, C], U8, tag="scales_" + name[0], align_bytes=64, name="scale_tile")
-                codes[name] = code_tile
-                scales[name] = scale_tile
-            cols = slice(256 * first, 256 * last)
+        def quantize(operand, first, last):
+            if operand not in codes:
+                code_tile = work.tile([P, C], U32, tag="codes_" + operand[0], align_bytes=64, name="code_tile")
+                scale_tile = work.tile([P, C], U8, tag="scales_" + operand[0], align_bytes=64, name="scale_tile")
+                codes[operand] = code_tile
+                scales[operand] = scale_tile
+            cols = slice(C // 4 * first, C // 4 * last)
             nc.vector.quantize_mx(
-                out=codes[name][:, cols].bitcast(E5M2X4),
-                scales=scales[name][:, cols],
-                in_=grouped[name][:, C * first : C * last],
+                out=codes[operand][:, cols].bitcast(E5M2X4),
+                scales=scales[operand][:, cols],
+                in_=interleaved[operand][:, C * first : C * last],
             )
 
-        def project(name, b, j, tag):
-            bank = psum.tile([P, N], F32, tag=tag, name="sums")
+        def project(operand, b, j, tag):
+            bank = psum.tile([P, N], F32, tag=tag, name="projected")
             for g in range(PASSES):
-                tok = slice((j * PASSES + g) * P, (j * PASSES + g + 1) * P)
-                ch = slice(g * N, (g + 1) * N)
+                tokens = slice((j * PASSES + g) * P, (j * PASSES + g + 1) * P)
+                channels = slice(g * N, (g + 1) * N)
                 nc.tensor.matmul_mx(
                     out=bank[:],
-                    lhsT=codes[("x", b)][:, tok].bitcast(E5M2X4),
-                    lhsT_scale=scales[("x", b)][:, tok],
-                    rhs=codes[name][:, ch].bitcast(E5M2X4),
-                    rhs_scale=scales[name][:, ch],
+                    lhsT=codes[("x", b)][:, tokens].bitcast(E5M2X4),
+                    lhsT_scale=scales[("x", b)][:, tokens],
+                    rhs=codes[operand][:, channels].bitcast(E5M2X4),
+                    rhs_scale=scales[operand][:, channels],
                     start=(g == 0),
                     stop=(g == PASSES - 1),
                 )
@@ -125,106 +126,151 @@ def tile_qwen3attention_pa_kernel(tc, x, cos, sin, wq, wk, wv, q_norm_w, k_norm_
         def place(s):
             return s // (B * J), (s // J) % B, s % J
 
-        sums = {}
+        main_banks = {}
         square_sums = {}
-        rstd = {}
+        inverse = {}
         products = {}
-        v_staged = {}
+        rotated = {}
+        values = {}
 
-        def project_qk(s):
+        def project_step(s):
             c, b, j = place(s)
-            sums[s] = project(("qk", c), b, j, "main")
+            main_banks[s] = project(("qk", c), b, j, "main")
 
-        def squares(s):
+        def sum_squares(s):
             ss = work.tile([P, HEADS], F32, tag="ss", bufs=4, name="ss")
             squared = work.tile([P, N], BF16, tag="squared", name="squared")
             for h in range(HEADS):
                 nc.scalar.activation(
                     out=squared[:, h * D : (h + 1) * D],
-                    in_=sums[s][:, h * D : (h + 1) * D],
+                    in_=main_banks[s][:, h * D : (h + 1) * D],
                     func=ACT.Square,
                     accum_out=ss[:, h : h + 1],
                 )
             square_sums[s] = ss
 
         def inverse_rms(s):
-            inv = work.tile([P, HEADS], F32, tag="rstd", bufs=4, name="inv")
+            inv = work.tile([P, HEADS], F32, tag="inverse", bufs=4, name="inv")
             nc.scalar.activation(
                 out=inv[:], in_=square_sums[s][:], func=ACT.Abs_reciprocal_sqrt, scale=1.0 / (D * EPS), bias=1.0
             )
-            rstd[s] = inv
+            inverse[s] = inv
 
         def multiply(s):
             c, b, j = place(s)
             if j == 0:
                 prod = work.tile([P, HEADS, J, 2, D], F32, tag="products", bufs=3, name="prod")
                 products[(c, b)] = prod
-            table = tables[0 if c < 4 else 1]
-            by_head = sums[s][:].rearrange("p (h d) -> p h d", h=HEADS)
+            table = tables[0 if c < Q_CHUNKS else 1]
+            by_head = main_banks[s][:].rearrange("p (h d) -> p h d", h=HEADS)
             for h in range(HEADS):
                 nc.vector.scalar_tensor_tensor(
                     out=products[(c, b)][:, h, j],
                     in0=by_head[:, h : h + 1, :].to_broadcast([P, 2, D]),
-                    scalar=rstd[s][:, h : h + 1],
+                    scalar=inverse[s][:, h : h + 1],
                     in1=table[:, j],
                     op0=ALU.mult,
                     op1=ALU.mult,
                 )
 
-        def hbm_heads(out, first_head, b):
-            return out[b, first_head : first_head + HEADS].rearrange("h (p j) d -> p h (j d)", j=J)
+        def add_terms(c, b, first, last, engine):
+            if (c, b) not in rotated:
+                done = work.tile([P, HEADS, J, D], F32, tag="rotated", bufs=3, name="done")
+                rotated[(c, b)] = done
+            terms = products[(c, b)][:, :, first:last].rearrange("p h j a (e i) -> p h (j a) e i", e=2)
+            total = rotated[(c, b)][:, :, first:last].rearrange("p h j (a i) -> p h (j a) i", a=2)
+            engine.tensor_tensor(out=total, in0=terms[:, :, :, 0, :], in1=terms[:, :, :, 1, :], op=ALU.add)
 
-        def add_and_store(c, b):
-            done = work.tile([P, HEADS, J * D], F32, tag="done", bufs=3, name="done")
-            terms = products[(c, b)][:].rearrange("p h j a (e i) -> p h (j a) e i", e=2)
-            total = done[:].rearrange("p h (m i) -> p h m i", i=HALF)
-            dst = hbm_heads(out_0, HEADS * c, b) if c < 4 else hbm_heads(out_1, HEADS * (c - 4), b)
-            if (c, b) == (QK_CHUNKS - 1, B - 1):
-                for h in range(HEADS):
-                    nc.vector.tensor_tensor(out=total[:, h], in0=terms[:, h, :, 0, :], in1=terms[:, h, :, 1, :], op=ALU.add)
-                    nc.sync.dma_start(out=dst[:, h, :], in_=done[:, h, :])
-            else:
-                nc.gpsimd.tensor_tensor(out=total, in0=terms[:, :, :, 0, :], in1=terms[:, :, :, 1, :], op=ALU.add)
-                nc.sync.dma_start(out=dst, in_=done[:])
+        def store(c, b, first, last):
+            dst = hbm_heads(out_0, c, b) if c < Q_CHUNKS else hbm_heads(out_1, c - Q_CHUNKS, b)
+            src = rotated[(c, b)][:].rearrange("p h j d -> p h (j d)")
+            nc.sync.dma_start(out=dst[:, :, first * D : last * D], in_=src[:, :, first * D : last * D])
+
+        adds_after = {s: (0, 1) for s in range(B * J - 2)}
+        adds_after[B * J - 1] = (0, 2)
+        fine_from = STEPS - 2 * J - 1
+        for s in range(B * J + J - 1, fine_from, J):
+            adds_after[s] = (0, J)
+        adds_after[fine_from] = (2, 2)
+        for s in range(fine_from + 2, STEPS - 3, 2):
+            adds_after[s] = (0, 2)
+        adds_after[STEPS - 3] = (1, 1)
+        adds_after[STEPS - 2] = (0, 1)
+        adds_after[STEPS - 1] = (1, 0)
+        waiting = []
+
+        def finish(s):
+            if s not in adds_after:
+                return
+            c, b, j = place(s)
+            while waiting:
+                store(*waiting[0])
+                waiting.remove(waiting[0])
+            on_vector, on_gpsimd = adds_after[s]
+            first = j + 1 - on_vector - on_gpsimd
+            if on_vector:
+                add_terms(c, b, first, first + on_vector, nc.vector)
+                store(c, b, first, first + on_vector)
+            if on_gpsimd:
+                add_terms(c, b, first + on_vector, j + 1, nc.gpsimd)
+                if s >= fine_from:
+                    waiting.append((c, b, first + on_vector, j + 1))
+                elif j == J - 1:
+                    waiting.append((c, b, 0, J))
 
         def produce(job):
-            if job[0] == "rows":
-                transpose_rows(job[1])
+            kind, what = job
+            if kind == "rows":
+                transpose_rows(what)
             else:
-                c, b, j = job[1]
-                banks[job] = project(("v", c), b, j, "side")
+                c, b, j = what
+                side_banks[what] = project(("v", c), b, j, "side")
 
         def consume(job):
-            if job[0] == "rows":
-                interleave(job[1])
+            kind, what = job
+            if kind == "rows":
+                interleave(what, nc.scalar.copy)
                 return
-            c, b, j = job[1]
+            c, b, j = what
             if j == 0:
-                values = work.tile([P, HEADS, J, D], F32, tag="values", name="values")
-                v_staged[(c, b)] = values
-            nc.scalar.copy(out=v_staged[(c, b)][:, :, j, :], in_=banks[job][:].rearrange("p (h d) -> p h d", h=HEADS))
+                gathered = work.tile([P, HEADS, J, D], F32, tag="values", name="gathered")
+                values[(c, b)] = gathered
+            nc.scalar.copy(out=values[(c, b)][:, :, j, :], in_=side_banks[what][:].rearrange("p (h d) -> p h d", h=HEADS))
             if j == J - 1:
-                nc.sync.dma_start(
-                    out=hbm_heads(out_2, HEADS * c, b), in_=v_staged[(c, b)][:].rearrange("p h j d -> p h (j d)")
-                )
+                nc.sync.dma_start(out=hbm_heads(out_2, c, b), in_=values[(c, b)][:].rearrange("p h j d -> p h (j d)"))
 
-        ident = const.tile([P, P], F32)
+        ident = const.tile([P, P], F32, name="ident")
         make_identity(nc, ident[:])
-        gain_row = const.tile([P, 2 * D], BF16)
-        ones = const.tile([P, P], BF16)
+        gain_row = const.tile([P, 2 * D], BF16, name="gain_row")
+        ones = const.tile([P, P], BF16, name="ones")
         nc.vector.memset(gain_row[:], 0.0)
         nc.vector.memset(ones[:], 1.0)
-        cos_sb = const.tile([P, J, HALF], BF16)
-        sin_sb = const.tile([P, J, HALF], BF16)
-        nc.scalar.dma_start(out=gain_row[0:1, 0:D], in_=q_norm_w.rearrange("(o d) -> o d", o=1))
-        nc.scalar.dma_start(out=gain_row[0:1, D : 2 * D], in_=k_norm_w.rearrange("(o d) -> o d", o=1))
-        nc.scalar.dma_start(out=cos_sb[:], in_=cos[0, 0].rearrange("(p j) f -> p j f", j=J))
-        nc.scalar.dma_start(out=sin_sb[:], in_=sin[0, 0].rearrange("(p j) f -> p j f", j=J))
-        for item in load_order[:ROW_BUFS]:
+        cos_sb = const.tile([P, J, HALF], BF16, name="cos_sb")
+        sin_sb = const.tile([P, J, HALF], BF16, name="sin_sb")
+        load_next()
+        nc.sync.dma_start(out=gain_row[0:1, 0:D], in_=q_norm_w.rearrange("(o d) -> o d", o=1))
+        nc.sync.dma_start(out=gain_row[0:1, D : 2 * D], in_=k_norm_w.rearrange("(o d) -> o d", o=1))
+        load_next()
+        load_next()
+        nc.sync.dma_start(out=cos_sb[:], in_=cos[0, 0].rearrange("(p j) f -> p j f", j=J))
+        nc.sync.dma_start(out=sin_sb[:], in_=sin[0, 0].rearrange("(p j) f -> p j f", j=J))
+        while len(loaded) < ROW_BUFS:
             load_next()
 
+        def turn(row_tile):
+            transpose_rows(row_tile)
+            interleave(row_tile, nc.scalar.copy)
+
+        def quantize_heads(pair):
+            for g in range(PASSES):
+                quantize(w0, 2 * g + pair, 2 * g + pair + 1)
+
+        turn((x0, 0))
+        quantize(x0, 0, 1)
+        turn((w0, 0))
         gains = psum.tile([P, 4, HALF], F32, tag="main", name="gains")
-        nc.tensor.matmul(gains[:].rearrange("p e i -> p (e i)"), lhsT=ones[:], rhs=gain_row[:], start=True, stop=True)
+        nc.tensor.matmul(gains[:].rearrange("p e i -> p (e i)"), lhsT=ones[:, 0:P], rhs=gain_row[:], start=True, stop=True)
+        turn((w0, 1))
         tables = []
         for which in range(2):
             table = const.tile([P, J, 2, D], F32, name="table%d" % which)
@@ -239,70 +285,63 @@ def tile_qwen3attention_pa_kernel(tc, x, cos, sin, wq, wk, wv, q_norm_w, k_norm_
                         op0=ALU.mult,
                         op1=ALU.mult,
                     )
-
-        x0, x1, w0 = ("x", 0), ("x", 1), ("qk", 0)
-        transpose_rows((x0, 0))
-        interleave((x0, 0))
-        quantize(x0, 0, 1)
-        for r in range(HEADS):
-            transpose_rows((w0, r))
-            interleave((w0, r), on_vector=(r % 2 == 1))
-        transpose_rows((x0, 1))
-        interleave((x0, 1))
-        quantize(w0, 0, 2)
-        quantize(w0, 2, 4)
+        quantize_heads(0)
+        turn((w0, 2))
+        turn((w0, 3))
+        quantize_heads(1)
+        turn((x0, 1))
+        turn((x0, 2))
+        project_step(0)
         quantize(x0, 1, 2)
-        project_qk(0)
-        project_qk(1)
-        for r in (2, 3):
-            transpose_rows((x0, r))
-            interleave((x0, r), on_vector=True)
-        quantize(x0, 2, 4)
+        quantize(x0, 2, 3)
 
-        jobs = {s: [] for s in range(-1, STEPS + 1)}
-        quantize_after = {0: (x1, 0, 2), 1: (x1, 2, 4)}
-        first = group(x1) + group(later[0])
-        for i, item in enumerate(first):
-            jobs[i // 2 - 1].append(("rows", item))
-        quantize_after[J - 1] = (later[0], 0, 4)
-        quads = [later[1], later[2], (0, 0), later[3], (0, 1), later[4], later[5], later[6], (1, 0), (1, 1)]
-        for q, what in enumerate(quads):
+        jobs = {s: [] for s in range(-1, STEPS + 2)}
+        for i, row_tile in enumerate(row_tiles(x0)[3:] + row_tiles(x1) + row_tiles(w1)):
+            jobs[i // 2 - 1].append(("rows", row_tile))
+        quantize_after = {0: (x0, 3, 4), 1: (x1, 0, 2), 2: (x1, 2, 4), 4: (w1, 0, 4)}
+        for q, what in enumerate(side_work):
+            start = J * (q + 1) - 1
             for i in range(J):
-                s = J * (q + 1) - 1 + i
                 if isinstance(what[0], str):
-                    jobs[s].append(("rows", (what, i)))
-                    quantize_after[J * (q + 2) - 1] = (what, 0, 4)
+                    jobs[start + i].append(("rows", (what, i)))
+                    quantize_after[start + J] = (what, 0, 4)
                 else:
-                    jobs[s].append(("v", (what[0], what[1], i)))
-
+                    jobs[start + i].append(("v", what + (i,)))
+        row_jobs = [job for s in sorted(jobs) for job in jobs[s] if job[0] == "rows"]
         made = set()
 
         def produce_for(s):
             for job in jobs[s]:
-                if job not in made:
-                    produce(job)
-                    made.add(job)
-                    if job[0] == "rows" and len(jobs[s]) == 1 and job[1][1] % 2 == 0:
-                        produce(jobs[s + 1][0])
-                        made.add(jobs[s + 1][0])
+                if job in made:
+                    continue
+                produce(job)
+                if job[0] == "rows" and job != row_jobs[-1]:
+                    partner = row_jobs[row_jobs.index(job) + 1]
+                    if partner in jobs[s] + jobs[s + 1]:
+                        produce(partner)
+                        made.add(partner)
 
         produce_for(-1)
-        for s in range(-1, STEPS):
-            if 2 <= s + 2 < STEPS:
-                project_qk(s + 2)
+        project_step(1)
+        produce_for(0)
+        sum_squares(0)
+        inverse_rms(0)
+        consume(jobs[-1][0])
+        interleave(jobs[-1][1][1], nc.vector.tensor_copy)
+
+        for s in range(STEPS):
+            if s + 2 < STEPS:
+                project_step(s + 2)
             produce_for(s + 1)
             if s + 1 < STEPS:
-                squares(s + 1)
+                sum_squares(s + 1)
             for job in jobs[s][:1]:
                 consume(job)
             if s + 1 < STEPS:
                 inverse_rms(s + 1)
             for job in jobs[s][1:]:
                 consume(job)
-            if s >= 0:
-                multiply(s)
-                if s in quantize_after:
-                    quantize(*quantize_after[s])
-                if s % J == J - 1:
-                    c, b, j = place(s)
-                    add_and_store(c, b)
+            multiply(s)
+            if s in quantize_after:
+                quantize(*quantize_after[s])
+            finish(s)

@@ -242,11 +242,22 @@ def tile_qwen3attention_pa_kernel(tc, x, cos, sin, wq, wk, wv, q_norm_w, k_norm_
         ident = const.tile([P, P], F32, name="ident")
         make_identity(nc, ident[:])
         gain_row = const.tile([P, 2 * D], BF16, name="gain_row")
-        ones = const.tile([P, P], BF16, name="ones")
+        ones = const.tile([P, N], BF16, name="ones")
         nc.vector.memset(gain_row[:], 0.0)
         nc.vector.memset(ones[:], 1.0)
         cos_sb = const.tile([P, J, HALF], BF16, name="cos_sb")
         sin_sb = const.tile([P, J, HALF], BF16, name="sin_sb")
+
+        unread = const.tile([P, 1], F32, name="unread")
+        nc.scalar.activation(out=unread[:], in_=ones[:, 0:1], func=ACT.Abs_reciprocal_sqrt)
+        unread_bank = psum.tile([P, N], F32, tag="main", name="unread_bank")
+
+        def warm_tensor(count):
+            for i in range(count):
+                nc.tensor.matmul(unread_bank[:], lhsT=ones[:, 0:P], rhs=ones[:], start=True, stop=True)
+
+        warm_tensor(4)
+
         load_next()
         nc.sync.dma_start(out=gain_row[0:1, 0:D], in_=q_norm_w.rearrange("(o d) -> o d", o=1))
         nc.sync.dma_start(out=gain_row[0:1, D : 2 * D], in_=k_norm_w.rearrange("(o d) -> o d", o=1))
@@ -270,6 +281,7 @@ def tile_qwen3attention_pa_kernel(tc, x, cos, sin, wq, wk, wv, q_norm_w, k_norm_
         turn((w0, 0))
         gains = psum.tile([P, 4, HALF], F32, tag="main", name="gains")
         nc.tensor.matmul(gains[:].rearrange("p e i -> p (e i)"), lhsT=ones[:, 0:P], rhs=gain_row[:], start=True, stop=True)
+        warm_tensor(2)
         turn((w0, 1))
         tables = []
         for which in range(2):
@@ -288,6 +300,7 @@ def tile_qwen3attention_pa_kernel(tc, x, cos, sin, wq, wk, wv, q_norm_w, k_norm_
         quantize_heads(0)
         turn((w0, 2))
         turn((w0, 3))
+        warm_tensor(2)
         quantize_heads(1)
         turn((x0, 1))
         turn((x0, 2))

@@ -189,9 +189,8 @@ def tile_qwen3attention_pa_kernel(tc, x, cos, sin, wq, wk, wv, q_norm_w, k_norm_
         adds_after = {s: (0, 1) for s in range(B * J - 2)}
         adds_after[B * J - 1] = (0, 2)
         fine_from = STEPS - 2 * J - 1
-        for s in range(B * J + J - 1, fine_from, J):
-            adds_after[s] = (0, J)
-        adds_after[fine_from] = (2, 2)
+        for s in range(B * J + 1, fine_from + 1, 2):
+            adds_after[s] = (0, 2)
         for s in range(fine_from + 2, STEPS - 3, 2):
             adds_after[s] = (0, 2)
         adds_after[STEPS - 3] = (1, 1)
@@ -213,7 +212,7 @@ def tile_qwen3attention_pa_kernel(tc, x, cos, sin, wq, wk, wv, q_norm_w, k_norm_
                 store(c, b, first, first + on_vector)
             if on_gpsimd:
                 add_terms(c, b, first + on_vector, j + 1, nc.gpsimd)
-                if s >= fine_from:
+                if s > fine_from:
                     waiting.append((c, b, first + on_vector, j + 1))
                 elif j == J - 1:
                     waiting.append((c, b, 0, J))
@@ -252,17 +251,14 @@ def tile_qwen3attention_pa_kernel(tc, x, cos, sin, wq, wk, wv, q_norm_w, k_norm_
         nc.scalar.activation(out=unread[:], in_=ones[:, 0:1], func=ACT.Abs_reciprocal_sqrt)
         unread_bank = psum.tile([P, N], F32, tag="main", name="unread_bank")
 
-        def warm_tensor(count):
-            for i in range(count):
-                nc.tensor.matmul(unread_bank[:], lhsT=ones[:, 0:P], rhs=ones[:], start=True, stop=True)
-
-        warm_tensor(4)
+        for i in range(4):
+            nc.tensor.matmul(unread_bank[:], lhsT=ones[:, 0:P], rhs=ones[:], start=True, stop=True)
 
         load_next()
         nc.sync.dma_start(out=gain_row[0:1, 0:D], in_=q_norm_w.rearrange("(o d) -> o d", o=1))
         nc.sync.dma_start(out=gain_row[0:1, D : 2 * D], in_=k_norm_w.rearrange("(o d) -> o d", o=1))
-        load_next()
-        load_next()
+        for r in range(2):
+            load_next()
         nc.sync.dma_start(out=cos_sb[:], in_=cos[0, 0].rearrange("(p j) f -> p j f", j=J))
         nc.sync.dma_start(out=sin_sb[:], in_=sin[0, 0].rearrange("(p j) f -> p j f", j=J))
         while len(loaded) < ROW_BUFS:
@@ -276,15 +272,9 @@ def tile_qwen3attention_pa_kernel(tc, x, cos, sin, wq, wk, wv, q_norm_w, k_norm_
             for g in range(PASSES):
                 quantize(w0, 2 * g + pair, 2 * g + pair + 1)
 
-        turn((x0, 0))
-        quantize(x0, 0, 1)
-        turn((w0, 0))
-        gains = psum.tile([P, 4, HALF], F32, tag="main", name="gains")
-        nc.tensor.matmul(gains[:].rearrange("p e i -> p (e i)"), lhsT=ones[:, 0:P], rhs=gain_row[:], start=True, stop=True)
-        warm_tensor(2)
-        turn((w0, 1))
         tables = []
-        for which in range(2):
+
+        def make_table(which):
             table = const.tile([P, J, 2, D], F32, name="table%d" % which)
             tables.append(table)
             for a in range(2):
@@ -297,16 +287,24 @@ def tile_qwen3attention_pa_kernel(tc, x, cos, sin, wq, wk, wv, q_norm_w, k_norm_
                         op0=ALU.mult,
                         op1=ALU.mult,
                     )
+
+        turn((x0, 0))
+        quantize(x0, 0, 1)
+        turn((w0, 0))
+        gains = psum.tile([P, 4, HALF], F32, tag="main", name="gains")
+        nc.tensor.matmul(gains[:].rearrange("p e i -> p (e i)"), lhsT=ones[:, 0:P], rhs=gain_row[:], start=True, stop=True)
+        turn((w0, 1))
+        make_table(0)
         quantize_heads(0)
         turn((w0, 2))
         turn((w0, 3))
-        warm_tensor(2)
         quantize_heads(1)
         turn((x0, 1))
         turn((x0, 2))
         project_step(0)
         quantize(x0, 1, 2)
         quantize(x0, 2, 3)
+        make_table(1)
 
         jobs = {s: [] for s in range(-1, STEPS + 2)}
         for i, row_tile in enumerate(row_tiles(x0)[3:] + row_tiles(x1) + row_tiles(w1)):

@@ -24,6 +24,7 @@ PASS_WORDS = 256
 HALF = D // 2
 Q_CHUNKS, K_CHUNKS, V_CHUNKS = 4, 2, 2
 STEPS = (Q_CHUNKS + K_CHUNKS) * B * J
+WARM_MATMULS = 4
 ROW_BUFS = 20
 
 
@@ -188,11 +189,10 @@ def tile_qwen3attention_pa_kernel(tc, x, cos, sin, wq, wk, wv, q_norm_w, k_norm_
 
         adds_after = {s: (0, 1) for s in range(B * J - 2)}
         adds_after[B * J - 1] = (0, 2)
-        fine_from = STEPS - 2 * J - 1
-        for s in range(B * J + 1, fine_from + 1, 2):
-            adds_after[s] = (0, 2)
-        for s in range(fine_from + 2, STEPS - 3, 2):
-            adds_after[s] = (0, 2)
+        fine_from = STEPS - J - 1
+        for s in range(B * J + J - 1, fine_from, J):
+            adds_after[s] = (0, J)
+        adds_after[fine_from] = (2, 2)
         adds_after[STEPS - 3] = (1, 1)
         adds_after[STEPS - 2] = (0, 1)
         adds_after[STEPS - 1] = (1, 0)
@@ -212,7 +212,7 @@ def tile_qwen3attention_pa_kernel(tc, x, cos, sin, wq, wk, wv, q_norm_w, k_norm_
                 store(c, b, first, first + on_vector)
             if on_gpsimd:
                 add_terms(c, b, first + on_vector, j + 1, nc.gpsimd)
-                if s > fine_from:
+                if s >= fine_from:
                     waiting.append((c, b, first + on_vector, j + 1))
                 elif j == J - 1:
                     waiting.append((c, b, 0, J))
@@ -251,7 +251,7 @@ def tile_qwen3attention_pa_kernel(tc, x, cos, sin, wq, wk, wv, q_norm_w, k_norm_
         nc.scalar.activation(out=unread[:], in_=ones[:, 0:1], func=ACT.Abs_reciprocal_sqrt)
         unread_bank = psum.tile([P, N], F32, tag="main", name="unread_bank")
 
-        for i in range(4):
+        for i in range(WARM_MATMULS):
             nc.tensor.matmul(unread_bank[:], lhsT=ones[:, 0:P], rhs=ones[:], start=True, stop=True)
 
         load_next()

from contextlib import ExitStack

import concourse.mybir as mybir
from concourse.masks import make_identity

B, T, C, D = 2, 512, 1024, 128
EPS = 1e-6
FLOPS = 2 * B * T * C * (16 + 8 + 8) * D

F32 = mybir.dt.float32
BF16 = mybir.dt.bfloat16
U32 = mybir.dt.uint32
U8 = mybir.dt.uint8
E5M2X4 = mybir.dt.float8_e5m2_x4
ACT = mybir.ActivationFunctionType
ALU = mybir.AluOpType

P = 128
J = T // P
HEADS = 4
N = HEADS * D
PASSES = C // 512
PASS_WORDS = 256
HALF = D // 2
Q_CHUNKS, K_CHUNKS, V_CHUNKS = 4, 2, 2
STEPS = (Q_CHUNKS + K_CHUNKS) * B * J
WARM_MATMULS = 4
ROW_BUFS = 20


def tile_qwen3attention_pa_kernel(tc, x, cos, sin, wq, wk, wv, q_norm_w, k_norm_w, out_0, out_1, out_2):
    nc = tc.nc
    with ExitStack() as ctx:
        const = ctx.enter_context(tc.tile_pool(name="const", bufs=1))
        work = ctx.enter_context(tc.tile_pool(name="work", bufs=2))
        psum = ctx.enter_context(tc.psum_pool(name="psum", bufs=4))
        ctx.enter_context(tc.manual_schedule())

        def row_tiles(operand):
            return [(operand, r) for r in range(4)]

        def hbm_rows(row_tile):
            (kind, i), r = row_tile
            if kind == "x":
                return x[i].rearrange("(p j) k -> p j k", j=J)[:, r, :]
            if kind == "v":
                return wv[i * N + r * D : i * N + (r + 1) * D, :]
            if i < Q_CHUNKS:
                return wq[i * N + r * D : i * N + (r + 1) * D, :]
            return wk[(i - Q_CHUNKS) * N + r * D : (i - Q_CHUNKS) * N + (r + 1) * D, :]

        def hbm_heads(out, chunk, b):
            return out[b, HEADS * chunk : HEADS * (chunk + 1)].rearrange("h (p j) d -> p h (j d)", j=J)

        x0, x1, w0, w1 = ("x", 0), ("x", 1), ("qk", 0), ("qk", 1)
        side_work = [("v", 0), ("qk", 2), (0, 0), ("qk", 3), ("v", 1), ("qk", 4), (0, 1), ("qk", 5), (1, 0), (1, 1)]
        load_order = row_tiles(x0)[:1] + row_tiles(w0) + row_tiles(x0)[1:] + row_tiles(x1) + row_tiles(w1)
        for what in side_work:
            if isinstance(what[0], str):
                load_order = load_order + row_tiles(what)

        loaded = {}
        side_banks = {}
        interleaved = {}
        codes = {}
        scales = {}

        def load_next():
            if len(loaded) < len(load_order):
                row_tile = load_order[len(loaded)]
                raw = work.tile([P, C], BF16, tag="rows", bufs=ROW_BUFS, name="raw")
                nc.sync.dma_start(out=raw[:], in_=hbm_rows(row_tile))
                loaded[row_tile] = raw

        def transpose_rows(row_tile):
            words = loaded[row_tile][:].bitcast(F32)
            bank = psum.tile([P, PASSES, 2, P], F32, tag="side", name="turned")
            for g in range(PASSES):
                for u in range(2):
                    nc.tensor.transpose(
                        bank[:, g, u, :], words[:, PASS_WORDS * g + u : PASS_WORDS * (g + 1) : 2], ident[:]
                    )
            side_banks[row_tile] = bank
            load_next()

        def interleave(row_tile, copy):
            operand, r = row_tile
            if operand not in interleaved:
                staged = work.tile([P, 4 * C], BF16, tag="interleaved", bufs=3, align_bytes=64, name="staged")
                interleaved[operand] = staged
            words = interleaved[operand][:].bitcast(F32)
            if operand[0] == "x":
                dst = words.rearrange("p (r g n u) -> p r g n u", r=4, g=PASSES, u=2)[:, r]
            else:
                dst = words.rearrange("p (g r n u) -> p g r n u", r=4, g=PASSES, u=2)[:, :, r]
            copy(out=dst, in_=side_banks[row_tile][:].rearrange("p g u n -> p g n u"))

        def quantize(operand, first, last):
            if operand not in codes:
                code_tile = work.tile([P, C], U32, tag="codes_" + operand[0], align_bytes=64, name="code_tile")
                scale_tile = work.tile([P, C], U8, tag="scales_" + operand[0], align_bytes=64, name="scale_tile")
                codes[operand] = code_tile
                scales[operand] = scale_tile
            cols = slice(C // 4 * first, C // 4 * last)
            nc.vector.quantize_mx(
                out=codes[operand][:, cols].bitcast(E5M2X4),
                scales=scales[operand][:, cols],
                in_=interleaved[operand][:, C * first : C * last],
            )

        def project(operand, b, j, tag):
            bank = psum.tile([P, N], F32, tag=tag, name="projected")
            for g in range(PASSES):
                tokens = slice((j * PASSES + g) * P, (j * PASSES + g + 1) * P)
                channels = slice(g * N, (g + 1) * N)
                nc.tensor.matmul_mx(
                    out=bank[:],
                    lhsT=codes[("x", b)][:, tokens].bitcast(E5M2X4),
                    lhsT_scale=scales[("x", b)][:, tokens],
                    rhs=codes[operand][:, channels].bitcast(E5M2X4),
                    rhs_scale=scales[operand][:, channels],
                    start=(g == 0),
                    stop=(g == PASSES - 1),
                )
            return bank

        def place(s):
            return s // (B * J), (s // J) % B, s % J

        main_banks = {}
        square_sums = {}
        inverse = {}
        products = {}
        rotated = {}
        values = {}

        def project_step(s):
            c, b, j = place(s)
            main_banks[s] = project(("qk", c), b, j, "main")

        def sum_squares(s):
            ss = work.tile([P, HEADS], F32, tag="ss", bufs=4, name="ss")
            squared = work.tile([P, N], BF16, tag="squared", name="squared")
            for h in range(HEADS):
                nc.scalar.activation(
                    out=squared[:, h * D : (h + 1) * D],
                    in_=main_banks[s][:, h * D : (h + 1) * D],
                    func=ACT.Square,
                    accum_out=ss[:, h : h + 1],
                )
            square_sums[s] = ss

        def inverse_rms(s):
            inv = work.tile([P, HEADS], F32, tag="inverse", bufs=4, name="inv")
            nc.scalar.activation(
                out=inv[:], in_=square_sums[s][:], func=ACT.Abs_reciprocal_sqrt, scale=1.0 / (D * EPS), bias=1.0
            )
            inverse[s] = inv

        def multiply(s):
            c, b, j = place(s)
            if j == 0:
                prod = work.tile([P, HEADS, J, 2, D], F32, tag="products", bufs=3, name="prod")
                products[(c, b)] = prod
            table = tables[0 if c < Q_CHUNKS else 1]
            by_head = main_banks[s][:].rearrange("p (h d) -> p h d", h=HEADS)
            for h in range(HEADS):
                nc.vector.scalar_tensor_tensor(
                    out=products[(c, b)][:, h, j],
                    in0=by_head[:, h : h + 1, :].to_broadcast([P, 2, D]),
                    scalar=inverse[s][:, h : h + 1],
                    in1=table[:, j],
                    op0=ALU.mult,
                    op1=ALU.mult,
                )

        def add_terms(c, b, first, last, engine):
            if (c, b) not in rotated:
                done = work.tile([P, HEADS, J, D], F32, tag="rotated", bufs=3, name="done")
                rotated[(c, b)] = done
            terms = products[(c, b)][:, :, first:last].rearrange("p h j a (e i) -> p h (j a) e i", e=2)
            total = rotated[(c, b)][:, :, first:last].rearrange("p h j (a i) -> p h (j a) i", a=2)
            engine.tensor_tensor(out=total, in0=terms[:, :, :, 0, :], in1=terms[:, :, :, 1, :], op=ALU.add)

        def store(c, b, first, last):
            dst = hbm_heads(out_0, c, b) if c < Q_CHUNKS else hbm_heads(out_1, c - Q_CHUNKS, b)
            src = rotated[(c, b)][:].rearrange("p h j d -> p h (j d)")
            nc.sync.dma_start(out=dst[:, :, first * D : last * D], in_=src[:, :, first * D : last * D])

        adds_after = {s: (0, 1) for s in range(B * J - 2)}
        adds_after[B * J - 1] = (0, 2)
        fine_from = STEPS - J - 1
        for s in range(B * J + J - 1, fine_from, J):
            adds_after[s] = (0, J)
        adds_after[fine_from] = (2, 2)
        adds_after[STEPS - 3] = (1, 1)
        adds_after[STEPS - 2] = (0, 1)
        adds_after[STEPS - 1] = (1, 0)
        waiting = []

        def finish(s):
            if s not in adds_after:
                return
            c, b, j = place(s)
            while waiting:
                store(*waiting[0])
                waiting.remove(waiting[0])
            on_vector, on_gpsimd = adds_after[s]
            first = j + 1 - on_vector - on_gpsimd
            if on_vector:
                add_terms(c, b, first, first + on_vector, nc.vector)
                store(c, b, first, first + on_vector)
            if on_gpsimd:
                add_terms(c, b, first + on_vector, j + 1, nc.gpsimd)
                if s >= fine_from:
                    waiting.append((c, b, first + on_vector, j + 1))
                elif j == J - 1:
                    waiting.append((c, b, 0, J))

        def produce(job):
            kind, what = job
            if kind == "rows":
                transpose_rows(what)
            else:
                c, b, j = what
                side_banks[what] = project(("v", c), b, j, "side")

        def consume(job):
            kind, what = job
            if kind == "rows":
                interleave(what, nc.scalar.copy)
                return
            c, b, j = what
            if j == 0:
                gathered = work.tile([P, HEADS, J, D], F32, tag="values", name="gathered")
                values[(c, b)] = gathered
            nc.scalar.copy(out=values[(c, b)][:, :, j, :], in_=side_banks[what][:].rearrange("p (h d) -> p h d", h=HEADS))
            if j == J - 1:
                nc.sync.dma_start(out=hbm_heads(out_2, c, b), in_=values[(c, b)][:].rearrange("p h j d -> p h (j d)"))

        ident = const.tile([P, P], F32, name="ident")
        make_identity(nc, ident[:])
        gain_row = const.tile([P, 2 * D], BF16, name="gain_row")
        ones = const.tile([P, N], BF16, name="ones")
        nc.vector.memset(gain_row[:], 0.0)
        nc.vector.memset(ones[:], 1.0)
        cos_sb = const.tile([P, J, HALF], BF16, name="cos_sb")
        sin_sb = const.tile([P, J, HALF], BF16, name="sin_sb")

        unread = const.tile([P, 1], F32, name="unread")
        nc.scalar.activation(out=unread[:], in_=ones[:, 0:1], func=ACT.Abs_reciprocal_sqrt)
        unread_bank = psum.tile([P, N], F32, tag="main", name="unread_bank")

        for i in range(WARM_MATMULS):
            nc.tensor.matmul(unread_bank[:], lhsT=ones[:, 0:P], rhs=ones[:], start=True, stop=True)

        load_next()
        nc.sync.dma_start(out=gain_row[0:1, 0:D], in_=q_norm_w.rearrange("(o d) -> o d", o=1))
        nc.sync.dma_start(out=gain_row[0:1, D : 2 * D], in_=k_norm_w.rearrange("(o d) -> o d", o=1))
        for r in range(2):
            load_next()
        nc.sync.dma_start(out=cos_sb[:], in_=cos[0, 0].rearrange("(p j) f -> p j f", j=J))
        nc.sync.dma_start(out=sin_sb[:], in_=sin[0, 0].rearrange("(p j) f -> p j f", j=J))
        while len(loaded) < ROW_BUFS:
            load_next()

        def turn(row_tile):
            transpose_rows(row_tile)
            interleave(row_tile, nc.scalar.copy)

        def quantize_heads(pair):
            for g in range(PASSES):
                quantize(w0, 2 * g + pair, 2 * g + pair + 1)

        tables = []

        def make_table(which):
            table = const.tile([P, J, 2, D], F32, name="table%d" % which)
            tables.append(table)
            for a in range(2):
                for e in range(2):
                    nc.vector.scalar_tensor_tensor(
                        out=table[:, :, a, e * HALF : (e + 1) * HALF],
                        in0=gains[:, 2 * which + e : 2 * which + e + 1, :].to_broadcast([P, J, HALF]),
                        scalar=(-1.0 if (a, e) == (0, 1) else 1.0) * EPS**-0.5,
                        in1=(cos_sb if a == e else sin_sb)[:],
                        op0=ALU.mult,
                        op1=ALU.mult,
                    )

        turn((x0, 0))
        quantize(x0, 0, 1)
        turn((w0, 0))
        gains = psum.tile([P, 4, HALF], F32, tag="main", name="gains")
        nc.tensor.matmul(gains[:].rearrange("p e i -> p (e i)"), lhsT=ones[:, 0:P], rhs=gain_row[:], start=True, stop=True)
        turn((w0, 1))
        make_table(0)
        quantize_heads(0)
        turn((w0, 2))
        turn((w0, 3))
        quantize_heads(1)
        turn((x0, 1))
        turn((x0, 2))
        project_step(0)
        quantize(x0, 1, 2)
        quantize(x0, 2, 3)
        make_table(1)

        jobs = {s: [] for s in range(-1, STEPS + 2)}
        for i, row_tile in enumerate(row_tiles(x0)[3:] + row_tiles(x1) + row_tiles(w1)):
            jobs[i // 2 - 1].append(("rows", row_tile))
        quantize_after = {0: (x0, 3, 4), 1: (x1, 0, 2), 2: (x1, 2, 4), 4: (w1, 0, 4)}
        for q, what in enumerate(side_work):
            start = J * (q + 1) - 1
            for i in range(J):
                if isinstance(what[0], str):
                    jobs[start + i].append(("rows", (what, i)))
                    quantize_after[start + J] = (what, 0, 4)
                else:
                    jobs[start + i].append(("v", what + (i,)))
        row_jobs = [job for s in sorted(jobs) for job in jobs[s] if job[0] == "rows"]
        made = set()

        def produce_for(s):
            for job in jobs[s]:
                if job in made:
                    continue
                produce(job)
                if job[0] == "rows" and job != row_jobs[-1]:
                    partner = row_jobs[row_jobs.index(job) + 1]
                    if partner in jobs[s] + jobs[s + 1]:
                        produce(partner)
                        made.add(partner)

        produce_for(-1)
        project_step(1)
        produce_for(0)
        sum_squares(0)
        inverse_rms(0)
        consume(jobs[-1][0])
        interleave(jobs[-1][1][1], nc.vector.tensor_copy)

        for s in range(STEPS):
            if s + 2 < STEPS:
                project_step(s + 2)
            produce_for(s + 1)
            if s + 1 < STEPS:
                sum_squares(s + 1)
            for job in jobs[s][:1]:
                consume(job)
            if s + 1 < STEPS:
                inverse_rms(s + 1)
            for job in jobs[s][1:]:
                consume(job)
            multiply(s)
            if s in quantize_after:
                quantize(*quantize_after[s])
            finish(s)
